import numpy as np
import ml_dtypes


def mxq(x, axis, fmt="e4m3"):
    dtype, down = {"e4m3": (ml_dtypes.float8_e4m3fn, 7), "e5m2": (ml_dtypes.float8_e5m2, 14)}[fmt]
    v = np.moveaxis(np.asarray(x, np.float32).astype(ml_dtypes.bfloat16).astype(np.float64), axis, -1)
    blocks = v.reshape(v.shape[:-1] + (-1, 32))
    amax = np.abs(blocks).max(-1, keepdims=True)
    byte = np.maximum(np.where(amax > 0, np.frexp(amax)[1] - 1 + 127, 0) - down, 1)
    scale = np.exp2(byte - 127.0)
    codes = (blocks / scale).astype(np.float32).astype(dtype).astype(np.float64)
    return np.moveaxis((codes * scale).reshape(v.shape), -1, axis)


WIDE = False


def mx_kscale(k):
    if not WIDE:
        return np.ones(k)
    levels = np.array([10, -10, 5, -5, 0])
    a = np.random.permutation(np.resize(levels, k // 512 * 4)).reshape(k // 512, 4)
    idx = np.arange(k)
    return np.exp2(a[idx // 512, idx % 128 // 32])


BF16 = ml_dtypes.bfloat16


def bf(x):
    return np.asarray(x, np.float32).astype(BF16)


def f64(x):
    return np.asarray(x).astype(np.float64)


N, DIN, DOUT, E, K, B = 512, 8, 64, 16, 3, 32
C = DIN + DOUT
ES = 2.8 / np.sqrt(E)


def sigmoid(v):
    return 1.0 / (1.0 + np.exp(-v))


def draw_adj():
    g = np.random.standard_normal((N, N))
    l = ES**2 * np.sqrt(E) * (g + g.T) / np.sqrt(2.0)
    idx = np.arange(N)
    l[idx, idx] = ES**2 * (E + np.sqrt(2.0 * E) * np.random.standard_normal(N))
    l = np.maximum(l, 0.0)
    e = np.exp(l - l.max(1, keepdims=True))
    return e / e.sum(1, keepdims=True)


def setup_inputs():
    s = mx_kscale(N)
    adj = draw_adj()
    cheb2 = 2.0 * draw_adj() - np.eye(N)
    return {"adj": bf(adj * s[None, :]),
            "cheb2": bf(cheb2 * s[None, :]),
            "x": bf(np.random.standard_normal((B, N, DIN)) / s[None, :, None]),
            "state": bf(np.random.standard_normal((B, N, DOUT)) / s[None, :, None]),
            "r_logit": bf(np.random.standard_normal((B, N, DOUT)) * 0.8)}


def reference(adj, cheb2, x, state, r_logit):
    r = sigmoid(f64(r_logit))
    cand = np.concatenate([f64(x), r * f64(state)], axis=-1)
    cq = mxq(cand, 1, "e4m3")
    agg1 = mxq(f64(adj), 1, "e4m3") @ cq
    agg2 = mxq(f64(cheb2), 1, "e4m3") @ cq
    return np.stack([agg1, agg2], axis=2)

@@ -1,0 +1,155 @@
+import concourse.masks as masks
+import concourse.mybir as mybir
+
+F32 = mybir.dt.float32
+BF16 = mybir.dt.bfloat16
+U32 = mybir.dt.uint32
+U8 = mybir.dt.uint8
+FP8X4 = mybir.dt.float8_e4m3fn_x4
+
+P = 128
+PACK = 4
+NODES = P * PACK
+BATCH = 32
+DIN = 8
+DOUT = 64
+FEAT = DIN + DOUT
+MATS = 2
+GROUP = 8
+GROUPS = BATCH // GROUP
+
+FLOPS = 2 * BATCH * NODES * NODES * MATS * FEAT
+
+
+def tile_agcrnlayer_pb_t_kernel(tc, adj, cheb2, x, state, r_logit, out):
+    nc = tc.nc
+    with tc.tile_pool(name="resident", bufs=1) as resident, tc.tile_pool(
+        name="rotating", bufs=2
+    ) as rotating, tc.psum_pool(name="banks", bufs=8) as banks:
+        mat_rows = resident.tile([P, MATS, PACK, NODES], BF16)
+        nc.sync.dma_start(out=mat_rows[:, 0], in_=adj.rearrange("(p r) n -> p r n", r=PACK))
+        nc.sync.dma_start(out=mat_rows[:, 1], in_=cheb2.rearrange("(p r) n -> p r n", r=PACK))
+        logit_rows = resident.tile([P, BATCH, PACK, DOUT], BF16)
+        state_rows = resident.tile([P, BATCH, PACK, DOUT], BF16)
+        x_rows = resident.tile([P, BATCH, PACK, DIN], BF16)
+        for g in range(GROUPS):
+            batches = slice(g * GROUP, (g + 1) * GROUP)
+            nc.sync.dma_start(
+                out=logit_rows[:, batches],
+                in_=r_logit[batches].rearrange("b (p t) c -> p b t c", t=PACK),
+            )
+            nc.sync.dma_start(
+                out=state_rows[:, batches],
+                in_=state[batches].rearrange("b (p t) c -> p b t c", t=PACK),
+            )
+            if g == 0:
+                nc.sync.dma_start(out=x_rows[:], in_=x.rearrange("b (p t) c -> p b t c", t=PACK))
+
+        ident = resident.tile([P, P], F32)
+        masks.make_identity(nc, ident[:])
+        mat_grouped = resident.tile([P, MATS, NODES, PACK], BF16, align_bytes=64)
+        mat_codes = resident.tile([P, MATS, NODES], U32, align_bytes=64)
+        mat_scales = resident.tile([P, MATS, NODES], U8, align_bytes=64)
+        for a in range(MATS):
+            for half in range(2):
+                flipped = banks.tile([P, 2, 2 * P], F32, tag="bank")
+                for r in (2 * half, 2 * half + 1):
+                    words = mat_rows[:, a, r, :].bitcast(F32).rearrange("p (w u) -> p u w", u=2)
+                    cols = slice((r % 2) * P, (r % 2 + 1) * P)
+                    for u in range(2):
+                        nc.tensor.transpose(flipped[:, u, cols], words[:, u, :], ident[:])
+                grouped_words = (
+                    mat_grouped[:, a, half * 2 * P : (half + 1) * 2 * P, :]
+                    .rearrange("p m t -> p (m t)")
+                    .bitcast(F32)
+                    .rearrange("p (m u) -> p m u", u=2)
+                )
+                nc.vector.tensor_copy(out=grouped_words, in_=flipped[:].rearrange("p u m -> p m u"))
+            nc.vector.quantize_mx(
+                out=mat_codes[:, a, :].bitcast(FP8X4),
+                scales=mat_scales[:, a, :],
+                in_=mat_grouped[:, a].rearrange("p m t -> p (m t)"),
+            )
+
+        out_rows = resident.tile([P, BATCH, PACK, MATS, FEAT], F32)
+
+        x_grouped = resident.tile([P, BATCH, DIN, PACK], BF16, align_bytes=64)
+        x_codes = resident.tile([P, BATCH * DIN], U32, align_bytes=64)
+        x_scales = resident.tile([P, BATCH * DIN], U8, align_bytes=64)
+        nc.vector.tensor_copy(out=x_grouped[:], in_=x_rows[:].rearrange("p b t c -> p b c t"))
+        nc.vector.quantize_mx(
+            out=x_codes[:].bitcast(FP8X4),
+            scales=x_scales[:],
+            in_=x_grouped[:].rearrange("p b c t -> p (b c t)"),
+        )
+        for r in range(PACK):
+            rows = slice(r * P, (r + 1) * P)
+            pair = banks.tile([P, MATS, BATCH * DIN], F32, tag="bank")
+            for a in range(MATS):
+                nc.tensor.matmul_mx(
+                    out=pair[:, a, :],
+                    lhsT=mat_codes[:, a, rows].bitcast(FP8X4),
+                    lhsT_scale=mat_scales[:, a, rows],
+                    rhs=x_codes[:].bitcast(FP8X4),
+                    rhs_scale=x_scales[:],
+                    start=True,
+                    stop=True,
+                )
+            nc.scalar.copy(
+                out=out_rows[:, :, r, :, 0:DIN],
+                in_=pair[:].rearrange("p a (b c) -> p b a c", c=DIN),
+            )
+
+        gated_codes = resident.tile([P, GROUPS, GROUP * DOUT], U32, align_bytes=64)
+        gated_scales = resident.tile([P, GROUPS, GROUP * DOUT], U8, align_bytes=64)
+
+        def quantise_gated_state(g):
+            batches = slice(g * GROUP, (g + 1) * GROUP)
+            gate = rotating.tile([P, GROUP, DOUT, PACK], F32)
+            nc.scalar.activation(
+                out=gate[:],
+                in_=logit_rows[:, batches].rearrange("p b t c -> p b c t"),
+                func=mybir.ActivationFunctionType.Sigmoid,
+            )
+            gated = rotating.tile([P, GROUP, DOUT, PACK], BF16, align_bytes=64)
+            nc.vector.tensor_tensor(
+                out=gated[:],
+                in0=gate[:],
+                in1=state_rows[:, batches].rearrange("p b t c -> p b c t"),
+                op=mybir.AluOpType.mult,
+            )
+            nc.vector.quantize_mx(
+                out=gated_codes[:, g, :].bitcast(FP8X4),
+                scales=gated_scales[:, g, :],
+                in_=gated[:].rearrange("p b c t -> p (b c t)"),
+            )
+
+        def aggregate(g):
+            batches = slice(g * GROUP, (g + 1) * GROUP)
+            for a in range(MATS):
+                for r in range(PACK):
+                    rows = slice(r * P, (r + 1) * P)
+                    acc = banks.tile([P, GROUP, DOUT], F32, tag="bank")
+                    nc.tensor.matmul_mx(
+                        out=acc[:].rearrange("p b c -> p (b c)"),
+                        lhsT=mat_codes[:, a, rows].bitcast(FP8X4),
+                        lhsT_scale=mat_scales[:, a, rows],
+                        rhs=gated_codes[:, g, :].bitcast(FP8X4),
+                        rhs_scale=gated_scales[:, g, :],
+                        start=True,
+                        stop=True,
+                    )
+                    if r % 2 == 0:
+                        nc.scalar.copy(out=out_rows[:, batches, r, a, DIN:FEAT], in_=acc[:])
+                    else:
+                        nc.vector.tensor_copy(out=out_rows[:, batches, r, a, DIN:FEAT], in_=acc[:])
+            nc.sync.dma_start(
+                out=out[batches].rearrange("b (p r) a c -> p b (r a c)", r=PACK),
+                in_=out_rows[:, batches].rearrange("p b r a c -> p b (r a c)"),
+            )
+
+        quantise_gated_state(0)
+        for g in range(GROUPS):
+            if g + 1 < GROUPS:
+                quantise_gated_state(g + 1)
+            aggregate(g)

@@ -15,8 +15,9 @@ DIN = 8
 DOUT = 64
 FEAT = DIN + DOUT
 MATS = 2
-GROUP = 8
+GROUP = 4
 GROUPS = BATCH // GROUP
+LOAD_BATCHES = 8
 
 FLOPS = 2 * BATCH * NODES * NODES * MATS * FEAT
 
@@ -25,25 +26,30 @@ def tile_agcrnlayer_pb_t_kernel(tc, adj, cheb2, x, state, r_logit, out):
     nc = tc.nc
     with tc.tile_pool(name="resident", bufs=1) as resident, tc.tile_pool(
         name="rotating", bufs=2
-    ) as rotating, tc.psum_pool(name="banks", bufs=8) as banks:
+    ) as rotating, tc.psum_pool(name="banks", bufs=8) as banks, tc.manual_schedule():
         mat_rows = resident.tile([P, MATS, PACK, NODES], BF16)
         nc.sync.dma_start(out=mat_rows[:, 0], in_=adj.rearrange("(p r) n -> p r n", r=PACK))
         nc.sync.dma_start(out=mat_rows[:, 1], in_=cheb2.rearrange("(p r) n -> p r n", r=PACK))
+        x_rows = resident.tile([P, BATCH, PACK, DIN], BF16)
+        nc.sync.dma_start(out=x_rows[:], in_=x.rearrange("b (p t) c -> p b t c", t=PACK))
         logit_rows = resident.tile([P, BATCH, PACK, DOUT], BF16)
         state_rows = resident.tile([P, BATCH, PACK, DOUT], BF16)
-        x_rows = resident.tile([P, BATCH, PACK, DIN], BF16)
-        for g in range(GROUPS):
-            batches = slice(g * GROUP, (g + 1) * GROUP)
+        for first in range(0, BATCH, LOAD_BATCHES):
+            loaded = slice(first, first + LOAD_BATCHES)
             nc.sync.dma_start(
-                out=logit_rows[:, batches],
-                in_=r_logit[batches].rearrange("b (p t) c -> p b t c", t=PACK),
+                out=logit_rows[:, loaded],
+                in_=r_logit[loaded].rearrange("b (p t) c -> p b t c", t=PACK),
             )
             nc.sync.dma_start(
-                out=state_rows[:, batches],
-                in_=state[batches].rearrange("b (p t) c -> p b t c", t=PACK),
+                out=state_rows[:, loaded],
+                in_=state[loaded].rearrange("b (p t) c -> p b t c", t=PACK),
             )
-            if g == 0:
-                nc.sync.dma_start(out=x_rows[:], in_=x.rearrange("b (p t) c -> p b t c", t=PACK))
+
+        def leave_psum(r, dst, src):
+            if r % 2 == 0:
+                nc.scalar.copy(out=dst, in_=src)
+            else:
+                nc.vector.tensor_copy(out=dst, in_=src)
 
         ident = resident.tile([P, P], F32)
         masks.make_identity(nc, ident[:])
@@ -64,12 +70,25 @@ def tile_agcrnlayer_pb_t_kernel(tc, adj, cheb2, x, state, r_logit, out):
                     .bitcast(F32)
                     .rearrange("p (m u) -> p m u", u=2)
                 )
-                nc.vector.tensor_copy(out=grouped_words, in_=flipped[:].rearrange("p u m -> p m u"))
+                nc.scalar.copy(out=grouped_words, in_=flipped[:].rearrange("p u m -> p m u"))
             nc.vector.quantize_mx(
                 out=mat_codes[:, a, :].bitcast(FP8X4),
                 scales=mat_scales[:, a, :],
                 in_=mat_grouped[:, a].rearrange("p m t -> p (m t)"),
             )
+
+        def multiply_by_matrices(bank, r, codes, scales):
+            rows = slice(r * P, (r + 1) * P)
+            for a in range(MATS):
+                nc.tensor.matmul_mx(
+                    out=bank[:, a, :],
+                    lhsT=mat_codes[:, a, rows].bitcast(FP8X4),
+                    lhsT_scale=mat_scales[:, a, rows],
+                    rhs=codes.bitcast(FP8X4),
+                    rhs_scale=scales,
+                    start=True,
+                    stop=True,
+                )
 
         out_rows = resident.tile([P, BATCH, PACK, MATS, FEAT], F32)
 
@@ -83,27 +102,18 @@ def tile_agcrnlayer_pb_t_kernel(tc, adj, cheb2, x, state, r_logit, out):
             in_=x_grouped[:].rearrange("p b c t -> p (b c t)"),
         )
         for r in range(PACK):
-            rows = slice(r * P, (r + 1) * P)
-            pair = banks.tile([P, MATS, BATCH * DIN], F32, tag="bank")
-            for a in range(MATS):
-                nc.tensor.matmul_mx(
-                    out=pair[:, a, :],
-                    lhsT=mat_codes[:, a, rows].bitcast(FP8X4),
-                    lhsT_scale=mat_scales[:, a, rows],
-                    rhs=x_codes[:].bitcast(FP8X4),
-                    rhs_scale=x_scales[:],
-                    start=True,
-                    stop=True,
-                )
-            nc.scalar.copy(
-                out=out_rows[:, :, r, :, 0:DIN],
-                in_=pair[:].rearrange("p a (b c) -> p b a c", c=DIN),
+            x_bank = banks.tile([P, MATS, BATCH * DIN], F32, tag="bank")
+            multiply_by_matrices(x_bank, r, x_codes[:], x_scales[:])
+            leave_psum(
+                r,
+                out_rows[:, :, r, :, 0:DIN],
+                x_bank[:].rearrange("p a (b c) -> p b a c", c=DIN),
             )
 
         gated_codes = resident.tile([P, GROUPS, GROUP * DOUT], U32, align_bytes=64)
         gated_scales = resident.tile([P, GROUPS, GROUP * DOUT], U8, align_bytes=64)
 
-        def quantise_gated_state(g):
+        def gate_state(g):
             batches = slice(g * GROUP, (g + 1) * GROUP)
             gate = rotating.tile([P, GROUP, DOUT, PACK], F32)
             nc.scalar.activation(
@@ -118,6 +128,9 @@ def tile_agcrnlayer_pb_t_kernel(tc, adj, cheb2, x, state, r_logit, out):
                 in1=state_rows[:, batches].rearrange("p b t c -> p b c t"),
                 op=mybir.AluOpType.mult,
             )
+            return gated
+
+        def quantise(g, gated):
             nc.vector.quantize_mx(
                 out=gated_codes[:, g, :].bitcast(FP8X4),
                 scales=gated_scales[:, g, :],
@@ -126,30 +139,27 @@ def tile_agcrnlayer_pb_t_kernel(tc, adj, cheb2, x, state, r_logit, out):
 
         def aggregate(g):
             batches = slice(g * GROUP, (g + 1) * GROUP)
-            for a in range(MATS):
-                for r in range(PACK):
-                    rows = slice(r * P, (r + 1) * P)
-                    acc = banks.tile([P, GROUP, DOUT], F32, tag="bank")
-                    nc.tensor.matmul_mx(
-                        out=acc[:].rearrange("p b c -> p (b c)"),
-                        lhsT=mat_codes[:, a, rows].bitcast(FP8X4),
-                        lhsT_scale=mat_scales[:, a, rows],
-                        rhs=gated_codes[:, g, :].bitcast(FP8X4),
-                        rhs_scale=gated_scales[:, g, :],
-                        start=True,
-                        stop=True,
-                    )
-                    if r % 2 == 0:
-                        nc.scalar.copy(out=out_rows[:, batches, r, a, DIN:FEAT], in_=acc[:])
-                    else:
-                        nc.vector.tensor_copy(out=out_rows[:, batches, r, a, DIN:FEAT], in_=acc[:])
+            for r in range(PACK):
+                bank = banks.tile([P, MATS, GROUP * DOUT], F32, tag="bank")
+                multiply_by_matrices(bank, r, gated_codes[:, g, :], gated_scales[:, g, :])
+                leave_psum(
+                    r,
+                    out_rows[:, batches, r, :, DIN:FEAT],
+                    bank[:].rearrange("p a (b c) -> p b a c", c=DOUT),
+                )
+
+        def store(g):
+            batches = slice(g * GROUP, (g + 1) * GROUP)
             nc.sync.dma_start(
                 out=out[batches].rearrange("b (p r) a c -> p b (r a c)", r=PACK),
                 in_=out_rows[:, batches].rearrange("p b r a c -> p b (r a c)"),
             )
 
-        quantise_gated_state(0)
+        quantise(0, gate_state(0))
         for g in range(GROUPS):
             if g + 1 < GROUPS:
-                quantise_gated_state(g + 1)
+                gated_next = gate_state(g + 1)
             aggregate(g)
+            if g + 1 < GROUPS:
+                quantise(g + 1, gated_next)
+            store(g)

@@ -25,8 +25,8 @@ FLOPS = 2 * BATCH * NODES * NODES * MATS * FEAT
 def tile_agcrnlayer_pb_t_kernel(tc, adj, cheb2, x, state, r_logit, out):
     nc = tc.nc
     with tc.tile_pool(name="resident", bufs=1) as resident, tc.tile_pool(
-        name="rotating", bufs=2
-    ) as rotating, tc.psum_pool(name="banks", bufs=8) as banks, tc.manual_schedule():
+        name="rotating", bufs=3
+    ) as rotating, tc.psum_pool(name="banks", bufs=8) as banks:
         mat_rows = resident.tile([P, MATS, PACK, NODES], BF16)
         nc.sync.dma_start(out=mat_rows[:, 0], in_=adj.rearrange("(p r) n -> p r n", r=PACK))
         nc.sync.dma_start(out=mat_rows[:, 1], in_=cheb2.rearrange("(p r) n -> p r n", r=PACK))
@@ -112,8 +112,10 @@ def tile_agcrnlayer_pb_t_kernel(tc, adj, cheb2, x, state, r_logit, out):
 
         gated_codes = resident.tile([P, GROUPS, GROUP * DOUT], U32, align_bytes=64)
         gated_scales = resident.tile([P, GROUPS, GROUP * DOUT], U8, align_bytes=64)
+        gates = {}
+        products = {}
 
-        def gate_state(g):
+        def open_gate(g):
             batches = slice(g * GROUP, (g + 1) * GROUP)
             gate = rotating.tile([P, GROUP, DOUT, PACK], F32)
             nc.scalar.activation(
@@ -121,23 +123,27 @@ def tile_agcrnlayer_pb_t_kernel(tc, adj, cheb2, x, state, r_logit, out):
                 in_=logit_rows[:, batches].rearrange("p b t c -> p b c t"),
                 func=mybir.ActivationFunctionType.Sigmoid,
             )
-            gated = rotating.tile([P, GROUP, DOUT, PACK], BF16, align_bytes=64)
+            gates[g] = gate
+
+        def gate_state(g):
+            batches = slice(g * GROUP, (g + 1) * GROUP)
+            product = rotating.tile([P, GROUP, DOUT, PACK], BF16, align_bytes=64)
             nc.vector.tensor_tensor(
-                out=gated[:],
-                in0=gate[:],
+                out=product[:],
+                in0=gates[g][:],
                 in1=state_rows[:, batches].rearrange("p b t c -> p b c t"),
                 op=mybir.AluOpType.mult,
             )
-            return gated
+            products[g] = product
 
-        def quantise(g, gated):
+        def quantise(g):
             nc.vector.quantize_mx(
                 out=gated_codes[:, g, :].bitcast(FP8X4),
                 scales=gated_scales[:, g, :],
-                in_=gated[:].rearrange("p b c t -> p (b c t)"),
+                in_=products[g][:].rearrange("p b c t -> p (b c t)"),
             )
 
-        def aggregate(g):
+        def aggregate_and_store(g):
             batches = slice(g * GROUP, (g + 1) * GROUP)
             for r in range(PACK):
                 bank = banks.tile([P, MATS, GROUP * DOUT], F32, tag="bank")
@@ -147,19 +153,17 @@ def tile_agcrnlayer_pb_t_kernel(tc, adj, cheb2, x, state, r_logit, out):
                     out_rows[:, batches, r, :, DIN:FEAT],
                     bank[:].rearrange("p a (b c) -> p b a c", c=DOUT),
                 )
-
-        def store(g):
-            batches = slice(g * GROUP, (g + 1) * GROUP)
             nc.sync.dma_start(
                 out=out[batches].rearrange("b (p r) a c -> p b (r a c)", r=PACK),
                 in_=out_rows[:, batches].rearrange("p b r a c -> p b (r a c)"),
             )
 
-        quantise(0, gate_state(0))
-        for g in range(GROUPS):
-            if g + 1 < GROUPS:
-                gated_next = gate_state(g + 1)
-            aggregate(g)
-            if g + 1 < GROUPS:
-                quantise(g + 1, gated_next)
-            store(g)
+        for step in range(GROUPS + 3):
+            if 3 <= step:
+                aggregate_and_store(step - 3)
+            if 2 <= step < GROUPS + 2:
+                quantise(step - 2)
+            if 1 <= step < GROUPS + 1:
+                gate_state(step - 1)
+            if step < GROUPS:
+                open_gate(step)

@@ -5,6 +5,7 @@ F32 = mybir.dt.float32
 BF16 = mybir.dt.bfloat16
 U32 = mybir.dt.uint32
 U8 = mybir.dt.uint8
+I32 = mybir.dt.int32
 FP8X4 = mybir.dt.float8_e4m3fn_x4
 
 P = 128
@@ -18,6 +19,7 @@ MATS = 2
 GROUP = 4
 GROUPS = BATCH // GROUP
 LOAD_BATCHES = 8
+SPREAD = P // BATCH
 
 FLOPS = 2 * BATCH * NODES * NODES * MATS * FEAT
 
@@ -30,8 +32,9 @@ def tile_agcrnlayer_pb_t_kernel(tc, adj, cheb2, x, state, r_logit, out):
         mat_rows = resident.tile([P, MATS, PACK, NODES], BF16)
         nc.sync.dma_start(out=mat_rows[:, 0], in_=adj.rearrange("(p r) n -> p r n", r=PACK))
         nc.sync.dma_start(out=mat_rows[:, 1], in_=cheb2.rearrange("(p r) n -> p r n", r=PACK))
-        x_rows = resident.tile([P, BATCH, PACK, DIN], BF16)
-        nc.sync.dma_start(out=x_rows[:], in_=x.rearrange("b (p t) c -> p b t c", t=PACK))
+        x_flat = resident.tile([P, NODES * DIN], BF16)
+        nc.vector.memset(x_flat[:].bitcast(I32), 0)
+        nc.sync.dma_start(out=x_flat[0:P:SPREAD, :], in_=x.rearrange("b n c -> b (n c)"))
         logit_rows = resident.tile([P, BATCH, PACK, DOUT], BF16)
         state_rows = resident.tile([P, BATCH, PACK, DOUT], BF16)
         for first in range(0, BATCH, LOAD_BATCHES):
@@ -95,7 +98,18 @@ def tile_agcrnlayer_pb_t_kernel(tc, adj, cheb2, x, state, r_logit, out):
         x_grouped = resident.tile([P, BATCH, DIN, PACK], BF16, align_bytes=64)
         x_codes = resident.tile([P, BATCH * DIN], U32, align_bytes=64)
         x_scales = resident.tile([P, BATCH * DIN], U8, align_bytes=64)
-        nc.vector.tensor_copy(out=x_grouped[:], in_=x_rows[:].rearrange("p b t c -> p b c t"))
+        x_words = x_flat[:].bitcast(F32).rearrange("q (p t w) -> q t w p", t=PACK, w=DIN // 2)
+        for w in range(DIN // 2):
+            flipped = banks.tile([P, PACK, P], F32, tag="bank")
+            for t in range(PACK):
+                nc.tensor.transpose(flipped[:, t, :], x_words[:, t, w, :], ident[:])
+            halves = (
+                flipped[:]
+                .rearrange("p t q -> p (t q)")
+                .bitcast(BF16)
+                .rearrange("p (t b s e) -> p s b e t", b=BATCH, s=SPREAD, e=2)
+            )
+            nc.vector.tensor_copy(out=x_grouped[:, :, 2 * w : 2 * w + 2, :], in_=halves[:, 0])
         nc.vector.quantize_mx(
             out=x_codes[:].bitcast(FP8X4),
             scales=x_scales[:],

@@ -16,8 +16,9 @@ DIN = 8
 DOUT = 64
 FEAT = DIN + DOUT
 MATS = 2
-GROUP = 4
-GROUPS = BATCH // GROUP
+COLS = 256
+GROUP = COLS // DOUT
+OPERANDS = 1 + BATCH // GROUP
 LOAD_BATCHES = 8
 SPREAD = P // BATCH
 
@@ -28,7 +29,7 @@ def tile_agcrnlayer_pb_t_kernel(tc, adj, cheb2, x, state, r_logit, out):
     nc = tc.nc
     with tc.tile_pool(name="resident", bufs=1) as resident, tc.tile_pool(
         name="rotating", bufs=3
-    ) as rotating, tc.psum_pool(name="banks", bufs=8) as banks:
+    ) as rotating, tc.psum_pool(name="banks", bufs=8) as banks, tc.manual_schedule():
         mat_rows = resident.tile([P, MATS, PACK, NODES], BF16)
         nc.sync.dma_start(out=mat_rows[:, 0], in_=adj.rearrange("(p r) n -> p r n", r=PACK))
         nc.sync.dma_start(out=mat_rows[:, 1], in_=cheb2.rearrange("(p r) n -> p r n", r=PACK))
@@ -47,12 +48,6 @@ def tile_agcrnlayer_pb_t_kernel(tc, adj, cheb2, x, state, r_logit, out):
                 out=state_rows[:, loaded],
                 in_=state[loaded].rearrange("b (p t) c -> p b t c", t=PACK),
             )
-
-        def leave_psum(r, dst, src):
-            if r % 2 == 0:
-                nc.scalar.copy(out=dst, in_=src)
-            else:
-                nc.vector.tensor_copy(out=dst, in_=src)
 
         ident = resident.tile([P, P], F32)
         masks.make_identity(nc, ident[:])
@@ -80,104 +75,102 @@ def tile_agcrnlayer_pb_t_kernel(tc, adj, cheb2, x, state, r_logit, out):
                 in_=mat_grouped[:, a].rearrange("p m t -> p (m t)"),
             )
 
-        def multiply_by_matrices(bank, r, codes, scales):
-            rows = slice(r * P, (r + 1) * P)
-            for a in range(MATS):
-                nc.tensor.matmul_mx(
-                    out=bank[:, a, :],
-                    lhsT=mat_codes[:, a, rows].bitcast(FP8X4),
-                    lhsT_scale=mat_scales[:, a, rows],
-                    rhs=codes.bitcast(FP8X4),
-                    rhs_scale=scales,
-                    start=True,
-                    stop=True,
-                )
-
+        cand_codes = resident.tile([P, OPERANDS, COLS], U32, align_bytes=64)
+        cand_scales = resident.tile([P, OPERANDS, COLS], U8, align_bytes=64)
         out_rows = resident.tile([P, BATCH, PACK, MATS, FEAT], F32)
-
-        x_grouped = resident.tile([P, BATCH, DIN, PACK], BF16, align_bytes=64)
-        x_codes = resident.tile([P, BATCH * DIN], U32, align_bytes=64)
-        x_scales = resident.tile([P, BATCH * DIN], U8, align_bytes=64)
-        x_words = x_flat[:].bitcast(F32).rearrange("q (p t w) -> q t w p", t=PACK, w=DIN // 2)
-        for w in range(DIN // 2):
-            flipped = banks.tile([P, PACK, P], F32, tag="bank")
-            for t in range(PACK):
-                nc.tensor.transpose(flipped[:, t, :], x_words[:, t, w, :], ident[:])
-            halves = (
-                flipped[:]
-                .rearrange("p t q -> p (t q)")
-                .bitcast(BF16)
-                .rearrange("p (t b s e) -> p s b e t", b=BATCH, s=SPREAD, e=2)
-            )
-            nc.vector.tensor_copy(out=x_grouped[:, :, 2 * w : 2 * w + 2, :], in_=halves[:, 0])
-        nc.vector.quantize_mx(
-            out=x_codes[:].bitcast(FP8X4),
-            scales=x_scales[:],
-            in_=x_grouped[:].rearrange("p b c t -> p (b c t)"),
-        )
-        for r in range(PACK):
-            x_bank = banks.tile([P, MATS, BATCH * DIN], F32, tag="bank")
-            multiply_by_matrices(x_bank, r, x_codes[:], x_scales[:])
-            leave_psum(
-                r,
-                out_rows[:, :, r, :, 0:DIN],
-                x_bank[:].rearrange("p a (b c) -> p b a c", c=DIN),
-            )
-
-        gated_codes = resident.tile([P, GROUPS, GROUP * DOUT], U32, align_bytes=64)
-        gated_scales = resident.tile([P, GROUPS, GROUP * DOUT], U8, align_bytes=64)
+        x_banks = []
         gates = {}
-        products = {}
+        grouped = {}
 
-        def open_gate(g):
-            batches = slice(g * GROUP, (g + 1) * GROUP)
-            gate = rotating.tile([P, GROUP, DOUT, PACK], F32)
-            nc.scalar.activation(
-                out=gate[:],
-                in_=logit_rows[:, batches].rearrange("p b t c -> p b c t"),
-                func=mybir.ActivationFunctionType.Sigmoid,
-            )
-            gates[g] = gate
+        def batches_of(i):
+            return slice((i - 1) * GROUP, i * GROUP)
 
-        def gate_state(g):
-            batches = slice(g * GROUP, (g + 1) * GROUP)
-            product = rotating.tile([P, GROUP, DOUT, PACK], BF16, align_bytes=64)
-            nc.vector.tensor_tensor(
-                out=product[:],
-                in0=gates[g][:],
-                in1=state_rows[:, batches].rearrange("p b t c -> p b c t"),
-                op=mybir.AluOpType.mult,
-            )
-            products[g] = product
-
-        def quantise(g):
-            nc.vector.quantize_mx(
-                out=gated_codes[:, g, :].bitcast(FP8X4),
-                scales=gated_scales[:, g, :],
-                in_=products[g][:].rearrange("p b c t -> p (b c t)"),
-            )
-
-        def aggregate_and_store(g):
-            batches = slice(g * GROUP, (g + 1) * GROUP)
-            for r in range(PACK):
-                bank = banks.tile([P, MATS, GROUP * DOUT], F32, tag="bank")
-                multiply_by_matrices(bank, r, gated_codes[:, g, :], gated_scales[:, g, :])
-                leave_psum(
-                    r,
-                    out_rows[:, batches, r, :, DIN:FEAT],
-                    bank[:].rearrange("p a (b c) -> p b a c", c=DOUT),
+        def prepare(i):
+            if i == 0:
+                x_words = x_flat[:].bitcast(F32).rearrange(
+                    "q (p t w) -> q t w p", t=PACK, w=DIN // 2
                 )
-            nc.sync.dma_start(
-                out=out[batches].rearrange("b (p r) a c -> p b (r a c)", r=PACK),
-                in_=out_rows[:, batches].rearrange("p b r a c -> p b (r a c)"),
+                for w in range(DIN // 2):
+                    flipped = banks.tile([P, PACK, P], F32, tag="bank")
+                    for t in range(PACK):
+                        nc.tensor.transpose(flipped[:, t, :], x_words[:, t, w, :], ident[:])
+                    x_banks.append(flipped)
+            else:
+                gate = rotating.tile([P, GROUP, DOUT, PACK], F32)
+                nc.scalar.activation(
+                    out=gate[:],
+                    in_=logit_rows[:, batches_of(i)].rearrange("p b t c -> p b c t"),
+                    func=mybir.ActivationFunctionType.Sigmoid,
+                )
+                gates[i] = gate
+
+        def group(i):
+            if i == 0:
+                x_grouped = resident.tile([P, BATCH, DIN, PACK], BF16, align_bytes=64)
+                for w in range(DIN // 2):
+                    halves = (
+                        x_banks[w][:]
+                        .rearrange("p t q -> p (t q)")
+                        .bitcast(BF16)
+                        .rearrange("p (t b s e) -> p s b e t", b=BATCH, s=SPREAD, e=2)
+                    )
+                    nc.vector.tensor_copy(
+                        out=x_grouped[:, :, 2 * w : 2 * w + 2, :], in_=halves[:, 0]
+                    )
+                grouped[i] = x_grouped
+            else:
+                product = rotating.tile([P, GROUP, DOUT, PACK], BF16, align_bytes=64)
+                nc.vector.tensor_tensor(
+                    out=product[:],
+                    in0=gates[i][:],
+                    in1=state_rows[:, batches_of(i)].rearrange("p b t c -> p b c t"),
+                    op=mybir.AluOpType.mult,
+                )
+                grouped[i] = product
+
+        def quantise(i):
+            nc.vector.quantize_mx(
+                out=cand_codes[:, i, :].bitcast(FP8X4),
+                scales=cand_scales[:, i, :],
+                in_=grouped[i][:].rearrange("p b c t -> p (b c t)"),
             )
 
-        for step in range(GROUPS + 3):
+        def aggregate(i):
+            for r in range(PACK):
+                rows = slice(r * P, (r + 1) * P)
+                bank = banks.tile([P, MATS, COLS], F32, tag="bank")
+                for a in range(MATS):
+                    nc.tensor.matmul_mx(
+                        out=bank[:, a, :],
+                        lhsT=mat_codes[:, a, rows].bitcast(FP8X4),
+                        lhsT_scale=mat_scales[:, a, rows],
+                        rhs=cand_codes[:, i, :].bitcast(FP8X4),
+                        rhs_scale=cand_scales[:, i, :],
+                        start=True,
+                        stop=True,
+                    )
+                if i == 0:
+                    dst = out_rows[:, :, r, :, 0:DIN]
+                    src = bank[:].rearrange("p a (b c) -> p b a c", c=DIN)
+                else:
+                    dst = out_rows[:, batches_of(i), r, :, DIN:FEAT]
+                    src = bank[:].rearrange("p a (b c) -> p b a c", c=DOUT)
+                if r % 2 == 0:
+                    nc.scalar.copy(out=dst, in_=src)
+                else:
+                    nc.vector.tensor_copy(out=dst, in_=src)
+            if i > 0:
+                nc.sync.dma_start(
+                    out=out[batches_of(i)].rearrange("b (p r) a c -> p b (r a c)", r=PACK),
+                    in_=out_rows[:, batches_of(i)].rearrange("p b r a c -> p b (r a c)"),
+                )
+
+        for step in range(OPERANDS + 3):
             if 3 <= step:
-                aggregate_and_store(step - 3)
-            if 2 <= step < GROUPS + 2:
+                aggregate(step - 3)
+            if 2 <= step < OPERANDS + 2:
                 quantise(step - 2)
-            if 1 <= step < GROUPS + 1:
-                gate_state(step - 1)
-            if step < GROUPS:
-                open_gate(step)
+            if 1 <= step < OPERANDS + 1:
+                group(step - 1)
+            if step < OPERANDS:
+                prepare(step)

@@ -30,6 +30,13 @@ def tile_agcrnlayer_pb_t_kernel(tc, adj, cheb2, x, state, r_logit, out):
     with tc.tile_pool(name="resident", bufs=1) as resident, tc.tile_pool(
         name="rotating", bufs=3
     ) as rotating, tc.psum_pool(name="banks", bufs=8) as banks, tc.manual_schedule():
+        warm = resident.tile([P, 1], F32)
+        warmed = resident.tile([P, 1], F32)
+        nc.gpsimd.memset(warm[:], 0.0)
+        nc.scalar.activation(
+            out=warmed[:], in_=warm[:], func=mybir.ActivationFunctionType.Sigmoid
+        )
+
         mat_rows = resident.tile([P, MATS, PACK, NODES], BF16)
         nc.sync.dma_start(out=mat_rows[:, 0], in_=adj.rearrange("(p r) n -> p r n", r=PACK))
         nc.sync.dma_start(out=mat_rows[:, 1], in_=cheb2.rearrange("(p r) n -> p r n", r=PACK))

@@ -162,7 +162,7 @@ def tile_agcrnlayer_pb_t_kernel(tc, adj, cheb2, x, state, r_logit, out):
                 else:
                     dst = out_rows[:, batches_of(i), r, :, DIN:FEAT]
                     src = bank[:].rearrange("p a (b c) -> p b a c", c=DOUT)
-                if r % 2 == 0:
+                if r % 2 == 0 or i == 0:
                     nc.scalar.copy(out=dst, in_=src)
                 else:
                     nc.vector.tensor_copy(out=dst, in_=src)

@@ -19,6 +19,7 @@ MATS = 2
 COLS = 256
 GROUP = COLS // DOUT
 OPERANDS = 1 + BATCH // GROUP
+LAST_PIECES = 2
 LOAD_BATCHES = 8
 SPREAD = P // BATCH
 
@@ -84,7 +85,7 @@ def tile_agcrnlayer_pb_t_kernel(tc, adj, cheb2, x, state, r_logit, out):
 
         cand_codes = resident.tile([P, OPERANDS, COLS], U32, align_bytes=64)
         cand_scales = resident.tile([P, OPERANDS, COLS], U8, align_bytes=64)
-        out_rows = resident.tile([P, BATCH, PACK, MATS, FEAT], F32)
+        out_rows = resident.tile([P, BATCH, PACK * MATS, FEAT], F32)
         x_banks = []
         gates = {}
         grouped = {}
@@ -143,34 +144,43 @@ def tile_agcrnlayer_pb_t_kernel(tc, adj, cheb2, x, state, r_logit, out):
             )
 
         def aggregate(i):
-            for r in range(PACK):
-                rows = slice(r * P, (r + 1) * P)
-                bank = banks.tile([P, MATS, COLS], F32, tag="bank")
-                for a in range(MATS):
-                    nc.tensor.matmul_mx(
-                        out=bank[:, a, :],
-                        lhsT=mat_codes[:, a, rows].bitcast(FP8X4),
-                        lhsT_scale=mat_scales[:, a, rows],
-                        rhs=cand_codes[:, i, :].bitcast(FP8X4),
-                        rhs_scale=cand_scales[:, i, :],
-                        start=True,
-                        stop=True,
+            pieces = LAST_PIECES if i == OPERANDS - 1 else 1
+            width = COLS // pieces
+            for piece in range(pieces):
+                cols = slice(piece * width, (piece + 1) * width)
+                if i > 0:
+                    first = (i - 1) * GROUP + piece * (GROUP // pieces)
+                    stored = slice(first, first + GROUP // pieces)
+                for r0 in range(0, PACK, pieces):
+                    bank = banks.tile([P, pieces * MATS, width], F32, tag="bank")
+                    for j in range(pieces):
+                        rows = slice((r0 + j) * P, (r0 + j + 1) * P)
+                        for a in range(MATS):
+                            nc.tensor.matmul_mx(
+                                out=bank[:, j * MATS + a, :],
+                                lhsT=mat_codes[:, a, rows].bitcast(FP8X4),
+                                lhsT_scale=mat_scales[:, a, rows],
+                                rhs=cand_codes[:, i, cols].bitcast(FP8X4),
+                                rhs_scale=cand_scales[:, i, cols],
+                                start=True,
+                                stop=True,
+                            )
+                    planes = slice(r0 * MATS, (r0 + pieces) * MATS)
+                    if i == 0:
+                        dst = out_rows[:, :, planes, 0:DIN]
+                        src = bank[:].rearrange("p q (b c) -> p b q c", c=DIN)
+                    else:
+                        dst = out_rows[:, stored, planes, DIN:FEAT]
+                        src = bank[:].rearrange("p q (b c) -> p b q c", c=DOUT)
+                    if (r0 // pieces) % 2 == 0 or i == 0:
+                        nc.scalar.copy(out=dst, in_=src)
+                    else:
+                        nc.vector.tensor_copy(out=dst, in_=src)
+                if i > 0:
+                    nc.sync.dma_start(
+                        out=out[stored].rearrange("b (p r) a c -> p b (r a c)", r=PACK),
+                        in_=out_rows[:, stored].rearrange("p b q c -> p b (q c)"),
                     )
-                if i == 0:
-                    dst = out_rows[:, :, r, :, 0:DIN]
-                    src = bank[:].rearrange("p a (b c) -> p b a c", c=DIN)
-                else:
-                    dst = out_rows[:, batches_of(i), r, :, DIN:FEAT]
-                    src = bank[:].rearrange("p a (b c) -> p b a c", c=DOUT)
-                if r % 2 == 0 or i == 0:
-                    nc.scalar.copy(out=dst, in_=src)
-                else:
-                    nc.vector.tensor_copy(out=dst, in_=src)
-            if i > 0:
-                nc.sync.dma_start(
-                    out=out[batches_of(i)].rearrange("b (p r) a c -> p b (r a c)", r=PACK),
-                    in_=out_rows[:, batches_of(i)].rearrange("p b r a c -> p b (r a c)"),
-                )
 
         for step in range(OPERANDS + 3):
             if 3 <= step:

@@ -143,51 +143,78 @@ def tile_agcrnlayer_pb_t_kernel(tc, adj, cheb2, x, state, r_logit, out):
                 in_=grouped[i][:].rearrange("p b c t -> p (b c t)"),
             )
 
-        def aggregate(i):
-            pieces = LAST_PIECES if i == OPERANDS - 1 else 1
-            width = COLS // pieces
-            for piece in range(pieces):
-                cols = slice(piece * width, (piece + 1) * width)
-                if i > 0:
-                    first = (i - 1) * GROUP + piece * (GROUP // pieces)
-                    stored = slice(first, first + GROUP // pieces)
-                for r0 in range(0, PACK, pieces):
-                    bank = banks.tile([P, pieces * MATS, width], F32, tag="bank")
-                    for j in range(pieces):
-                        rows = slice((r0 + j) * P, (r0 + j + 1) * P)
-                        for a in range(MATS):
-                            nc.tensor.matmul_mx(
-                                out=bank[:, j * MATS + a, :],
-                                lhsT=mat_codes[:, a, rows].bitcast(FP8X4),
-                                lhsT_scale=mat_scales[:, a, rows],
-                                rhs=cand_codes[:, i, cols].bitcast(FP8X4),
-                                rhs_scale=cand_scales[:, i, cols],
-                                start=True,
-                                stop=True,
-                            )
-                    planes = slice(r0 * MATS, (r0 + pieces) * MATS)
-                    if i == 0:
-                        dst = out_rows[:, :, planes, 0:DIN]
-                        src = bank[:].rearrange("p q (b c) -> p b q c", c=DIN)
-                    else:
-                        dst = out_rows[:, stored, planes, DIN:FEAT]
-                        src = bank[:].rearrange("p q (b c) -> p b q c", c=DOUT)
-                    if (r0 // pieces) % 2 == 0 or i == 0:
-                        nc.scalar.copy(out=dst, in_=src)
-                    else:
-                        nc.vector.tensor_copy(out=dst, in_=src)
-                if i > 0:
-                    nc.sync.dma_start(
-                        out=out[stored].rearrange("b (p r) a c -> p b (r a c)", r=PACK),
-                        in_=out_rows[:, stored].rearrange("p b q c -> p b (q c)"),
-                    )
+        products = {}
+        BANKS = PACK
 
-        for step in range(OPERANDS + 3):
-            if 3 <= step:
-                aggregate(step - 3)
-            if 2 <= step < OPERANDS + 2:
-                quantise(step - 2)
-            if 1 <= step < OPERANDS + 1:
-                group(step - 1)
+        def pieces_of(i):
+            return LAST_PIECES if i == OPERANDS - 1 else 1
+
+        def multiply(i):
+            pieces = pieces_of(i)
+            width = COLS // pieces
+            products[i] = []
+            for k in range(BANKS):
+                piece, r0 = divmod(k * pieces, PACK)
+                cols = slice(piece * width, (piece + 1) * width)
+                bank = banks.tile([P, pieces * MATS, width], F32, tag="bank")
+                for j in range(pieces):
+                    rows = slice((r0 + j) * P, (r0 + j + 1) * P)
+                    for a in range(MATS):
+                        nc.tensor.matmul_mx(
+                            out=bank[:, j * MATS + a, :],
+                            lhsT=mat_codes[:, a, rows].bitcast(FP8X4),
+                            lhsT_scale=mat_scales[:, a, rows],
+                            rhs=cand_codes[:, i, cols].bitcast(FP8X4),
+                            rhs_scale=cand_scales[:, i, cols],
+                            start=True,
+                            stop=True,
+                        )
+                products[i].append(bank)
+
+        def stored_batches(i, piece):
+            count = GROUP // pieces_of(i)
+            first = (i - 1) * GROUP + piece * count
+            return slice(first, first + count)
+
+        def empty(i, k):
+            pieces = pieces_of(i)
+            piece, r0 = divmod(k * pieces, PACK)
+            bank = products[i][k]
+            planes = slice(r0 * MATS, (r0 + pieces) * MATS)
+            if i == 0:
+                dst = out_rows[:, :, planes, 0:DIN]
+                src = bank[:].rearrange("p q (b c) -> p b q c", c=DIN)
+            else:
+                dst = out_rows[:, stored_batches(i, piece), planes, DIN:FEAT]
+                src = bank[:].rearrange("p q (b c) -> p b q c", c=DOUT)
+            if k % 2 == 0 or i == 0:
+                nc.scalar.copy(out=dst, in_=src)
+            else:
+                nc.vector.tensor_copy(out=dst, in_=src)
+
+        def store(i, piece):
+            stored = stored_batches(i, piece)
+            nc.sync.dma_start(
+                out=out[stored].rearrange("b (p r) a c -> p b (r a c)", r=PACK),
+                in_=out_rows[:, stored].rearrange("p b q c -> p b (q c)"),
+            )
+
+        prepare(0)
+        for step in range(OPERANDS + 1):
             if step < OPERANDS:
-                prepare(step)
+                group(step)
+            if step + 1 < OPERANDS:
+                prepare(step + 1)
+            if step >= 1:
+                empty(step - 1, 0)
+                empty(step - 1, 1)
+                if step >= 2 and pieces_of(step - 1) == 2:
+                    store(step - 1, 0)
+            if step < OPERANDS:
+                quantise(step)
+                multiply(step)
+            if step >= 1:
+                empty(step - 1, 2)
+                empty(step - 1, 3)
+            if step >= 2:
+                store(step - 1, pieces_of(step - 1) - 1)

@@ -20,6 +20,7 @@ COLS = 256
 GROUP = COLS // DOUT
 OPERANDS = 1 + BATCH // GROUP
 LAST_PIECES = 2
+WARM_COLS = 512
 LOAD_BATCHES = 8
 SPREAD = P // BATCH
 
@@ -37,6 +38,18 @@ def tile_agcrnlayer_pb_t_kernel(tc, adj, cheb2, x, state, r_logit, out):
         nc.scalar.activation(
             out=warmed[:], in_=warm[:], func=mybir.ActivationFunctionType.Sigmoid
         )
+
+        zeros = resident.tile([P, WARM_COLS], BF16)
+        nc.vector.memset(zeros[:], 0.0)
+
+        def keep_warm(count):
+            unused = banks.tile([P, WARM_COLS], F32, tag="bank")
+            for repeat in range(count):
+                nc.tensor.matmul(
+                    out=unused[:], lhsT=zeros[:, 0:P], rhs=zeros[:], start=True, stop=True
+                )
+
+        keep_warm(5)
 
         mat_rows = resident.tile([P, MATS, PACK, NODES], BF16)
         nc.sync.dma_start(out=mat_rows[:, 0], in_=adj.rearrange("(p r) n -> p r n", r=PACK))
@@ -77,6 +90,7 @@ def tile_agcrnlayer_pb_t_kernel(tc, adj, cheb2, x, state, r_logit, out):
                     .rearrange("p (m u) -> p m u", u=2)
                 )
                 nc.scalar.copy(out=grouped_words, in_=flipped[:].rearrange("p u m -> p m u"))
+            keep_warm(2)
             nc.vector.quantize_mx(
                 out=mat_codes[:, a, :].bitcast(FP8X4),
                 scales=mat_scales[:, a, :],
@@ -103,6 +117,8 @@ def tile_agcrnlayer_pb_t_kernel(tc, adj, cheb2, x, state, r_logit, out):
                     for t in range(PACK):
                         nc.tensor.transpose(flipped[:, t, :], x_words[:, t, w, :], ident[:])
                     x_banks.append(flipped)
+                    if w % 2 == 1:
+                        keep_warm(2)
             else:
                 gate = rotating.tile([P, GROUP, DOUT, PACK], F32)
                 nc.scalar.activation(

@@ -21,7 +21,7 @@ GROUP = COLS // DOUT
 OPERANDS = 1 + BATCH // GROUP
 LAST_PIECES = 2
 WARM_COLS = 512
-LOAD_BATCHES = 8
+LOAD_BOUNDS = (0, 4, 8, 16, 24, 32)
 SPREAD = P // BATCH
 
 FLOPS = 2 * BATCH * NODES * NODES * MATS * FEAT
@@ -52,15 +52,18 @@ def tile_agcrnlayer_pb_t_kernel(tc, adj, cheb2, x, state, r_logit, out):
         keep_warm(5)
 
         mat_rows = resident.tile([P, MATS, PACK, NODES], BF16)
-        nc.sync.dma_start(out=mat_rows[:, 0], in_=adj.rearrange("(p r) n -> p r n", r=PACK))
-        nc.sync.dma_start(out=mat_rows[:, 1], in_=cheb2.rearrange("(p r) n -> p r n", r=PACK))
+        for a, matrix in enumerate((adj, cheb2)):
+            rows_of = matrix.rearrange("(p r) n -> p r n", r=PACK)
+            for half in range(2):
+                pair = slice(2 * half, 2 * half + 2)
+                nc.sync.dma_start(out=mat_rows[:, a, pair], in_=rows_of[:, pair])
         x_flat = resident.tile([P, NODES * DIN], BF16)
         nc.vector.memset(x_flat[:].bitcast(I32), 0)
         nc.sync.dma_start(out=x_flat[0:P:SPREAD, :], in_=x.rearrange("b n c -> b (n c)"))
         logit_rows = resident.tile([P, BATCH, PACK, DOUT], BF16)
         state_rows = resident.tile([P, BATCH, PACK, DOUT], BF16)
-        for first in range(0, BATCH, LOAD_BATCHES):
-            loaded = slice(first, first + LOAD_BATCHES)
+        for first, behind in zip(LOAD_BOUNDS[:-1], LOAD_BOUNDS[1:]):
+            loaded = slice(first, behind)
             nc.sync.dma_start(
                 out=logit_rows[:, loaded],
                 in_=r_logit[loaded].rearrange("b (p t) c -> p b t c", t=PACK),
@@ -89,7 +92,12 @@ def tile_agcrnlayer_pb_t_kernel(tc, adj, cheb2, x, state, r_logit, out):
                     .bitcast(F32)
                     .rearrange("p (m u) -> p m u", u=2)
                 )
-                nc.scalar.copy(out=grouped_words, in_=flipped[:].rearrange("p u m -> p m u"))
+                if half == 0:
+                    nc.scalar.copy(out=grouped_words, in_=flipped[:].rearrange("p u m -> p m u"))
+                else:
+                    nc.vector.tensor_copy(
+                        out=grouped_words, in_=flipped[:].rearrange("p u m -> p m u")
+                    )
             keep_warm(2)
             nc.vector.quantize_mx(
                 out=mat_codes[:, a, :].bitcast(FP8X4),
@@ -117,7 +125,7 @@ def tile_agcrnlayer_pb_t_kernel(tc, adj, cheb2, x, state, r_logit, out):
                     for t in range(PACK):
                         nc.tensor.transpose(flipped[:, t, :], x_words[:, t, w, :], ident[:])
                     x_banks.append(flipped)
-                    if w % 2 == 1:
+                    if w == 1:
                         keep_warm(2)
             else:
                 gate = rotating.tile([P, GROUP, DOUT, PACK], F32)
@@ -128,29 +136,27 @@ def tile_agcrnlayer_pb_t_kernel(tc, adj, cheb2, x, state, r_logit, out):
                 )
                 gates[i] = gate
 
+        x_grouped = resident.tile([P, BATCH, DIN, PACK], BF16, align_bytes=64)
+        grouped[0] = x_grouped
+
+        def group_x(w, copy):
+            halves = (
+                x_banks[w][:]
+                .rearrange("p t q -> p (t q)")
+                .bitcast(BF16)
+                .rearrange("p (t b s e) -> p s b e t", b=BATCH, s=SPREAD, e=2)
+            )
+            copy(out=x_grouped[:, :, 2 * w : 2 * w + 2, :], in_=halves[:, 0])
+
         def group(i):
-            if i == 0:
-                x_grouped = resident.tile([P, BATCH, DIN, PACK], BF16, align_bytes=64)
-                for w in range(DIN // 2):
-                    halves = (
-                        x_banks[w][:]
-                        .rearrange("p t q -> p (t q)")
-                        .bitcast(BF16)
-                        .rearrange("p (t b s e) -> p s b e t", b=BATCH, s=SPREAD, e=2)
-                    )
-                    nc.vector.tensor_copy(
-                        out=x_grouped[:, :, 2 * w : 2 * w + 2, :], in_=halves[:, 0]
-                    )
-                grouped[i] = x_grouped
-            else:
-                product = rotating.tile([P, GROUP, DOUT, PACK], BF16, align_bytes=64)
-                nc.vector.tensor_tensor(
-                    out=product[:],
-                    in0=gates[i][:],
-                    in1=state_rows[:, batches_of(i)].rearrange("p b t c -> p b c t"),
-                    op=mybir.AluOpType.mult,
-                )
-                grouped[i] = product
+            product = rotating.tile([P, GROUP, DOUT, PACK], BF16, align_bytes=64)
+            nc.vector.tensor_tensor(
+                out=product[:],
+                in0=gates[i][:],
+                in1=state_rows[:, batches_of(i)].rearrange("p b t c -> p b c t"),
+                op=mybir.AluOpType.mult,
+            )
+            grouped[i] = product
 
         def quantise(i):
             nc.vector.quantize_mx(
@@ -203,7 +209,7 @@ def tile_agcrnlayer_pb_t_kernel(tc, adj, cheb2, x, state, r_logit, out):
             else:
                 dst = out_rows[:, stored_batches(i, piece), planes, DIN:FEAT]
                 src = bank[:].rearrange("p q (b c) -> p b q c", c=DOUT)
-            if k % 2 == 0 or i == 0:
+            if k % 2 == 0:
                 nc.scalar.copy(out=dst, in_=src)
             else:
                 nc.vector.tensor_copy(out=dst, in_=src)
@@ -216,21 +222,38 @@ def tile_agcrnlayer_pb_t_kernel(tc, adj, cheb2, x, state, r_logit, out):
             )
 
         prepare(0)
-        for step in range(OPERANDS + 1):
+        prepare(1)
+        group(1)
+        group_x(0, nc.scalar.copy)
+        group_x(1, nc.scalar.copy)
+        group_x(2, nc.vector.tensor_copy)
+        quantise(1)
+        multiply(1)
+        group_x(3, nc.vector.tensor_copy)
+        prepare(2)
+        quantise(0)
+        multiply(0)
+        group(2)
+        for i in (1, 0):
+            for k in range(BANKS):
+                empty(i, k)
+        store(1, 0)
+        prepare(3)
+        quantise(2)
+        multiply(2)
+
+        for step in range(3, OPERANDS + 1):
             if step < OPERANDS:
                 group(step)
             if step + 1 < OPERANDS:
                 prepare(step + 1)
-            if step >= 1:
-                empty(step - 1, 0)
-                empty(step - 1, 1)
-                if step >= 2 and pieces_of(step - 1) == 2:
-                    store(step - 1, 0)
+            empty(step - 1, 0)
+            empty(step - 1, 1)
+            if pieces_of(step - 1) == 2:
+                store(step - 1, 0)
             if step < OPERANDS:
                 quantise(step)
                 multiply(step)
-            if step >= 1:
-                empty(step - 1, 2)
-                empty(step - 1, 3)
-            if step >= 2:
-                store(step - 1, pieces_of(step - 1) - 1)
+            empty(step - 1, 2)
+            empty(step - 1, 3)
+            store(step - 1, pieces_of(step - 1) - 1)

@@ -209,7 +209,7 @@ def tile_agcrnlayer_pb_t_kernel(tc, adj, cheb2, x, state, r_logit, out):
             else:
                 dst = out_rows[:, stored_batches(i, piece), planes, DIN:FEAT]
                 src = bank[:].rearrange("p q (b c) -> p b q c", c=DOUT)
-            if k % 2 == 0:
+            if k % 2 == 0 or (k == 3 and i in (2, 4, 6)):
                 nc.scalar.copy(out=dst, in_=src)
             else:
                 nc.vector.tensor_copy(out=dst, in_=src)

@@ -23,6 +23,7 @@ LAST_PIECES = 2
 WARM_COLS = 512
 LOAD_BOUNDS = (0, 4, 8, 16, 24, 32)
 SPREAD = P // BATCH
+DMA_ALIGN = 256
 
 FLOPS = 2 * BATCH * NODES * NODES * MATS * FEAT
 
@@ -51,17 +52,17 @@ def tile_agcrnlayer_pb_t_kernel(tc, adj, cheb2, x, state, r_logit, out):
 
         keep_warm(5)
 
-        mat_rows = resident.tile([P, MATS, PACK, NODES], BF16)
+        mat_rows = resident.tile([P, MATS, PACK, NODES], BF16, align_bytes=DMA_ALIGN)
         for a, matrix in enumerate((adj, cheb2)):
             rows_of = matrix.rearrange("(p r) n -> p r n", r=PACK)
             for half in range(2):
                 pair = slice(2 * half, 2 * half + 2)
                 nc.sync.dma_start(out=mat_rows[:, a, pair], in_=rows_of[:, pair])
-        x_flat = resident.tile([P, NODES * DIN], BF16)
+        x_flat = resident.tile([P, NODES * DIN], BF16, align_bytes=DMA_ALIGN)
         nc.vector.memset(x_flat[:].bitcast(I32), 0)
         nc.sync.dma_start(out=x_flat[0:P:SPREAD, :], in_=x.rearrange("b n c -> b (n c)"))
-        logit_rows = resident.tile([P, BATCH, PACK, DOUT], BF16)
-        state_rows = resident.tile([P, BATCH, PACK, DOUT], BF16)
+        logit_rows = resident.tile([P, BATCH, PACK, DOUT], BF16, align_bytes=DMA_ALIGN)
+        state_rows = resident.tile([P, BATCH, PACK, DOUT], BF16, align_bytes=DMA_ALIGN)
         for first, behind in zip(LOAD_BOUNDS[:-1], LOAD_BOUNDS[1:]):
             loaded = slice(first, behind)
             nc.sync.dma_start(
@@ -107,7 +108,9 @@ def tile_agcrnlayer_pb_t_kernel(tc, adj, cheb2, x, state, r_logit, out):
 
         cand_codes = resident.tile([P, OPERANDS, COLS], U32, align_bytes=64)
         cand_scales = resident.tile([P, OPERANDS, COLS], U8, align_bytes=64)
-        out_rows = resident.tile([P, BATCH, PACK * MATS, FEAT], F32)
+        out_rows = resident.tile(
+            [P, BATCH, PACK * MATS, FEAT], F32, align_bytes=DMA_ALIGN
+        )
         x_banks = []
         gates = {}
         grouped = {}

@@ -23,7 +23,7 @@ LAST_PIECES = 2
 WARM_COLS = 512
 LOAD_BOUNDS = (0, 4, 8, 16, 24, 32)
 SPREAD = P // BATCH
-DMA_ALIGN = 256
+DMA_ALIGN = 4096
 
 FLOPS = 2 * BATCH * NODES * NODES * MATS * FEAT
 

@@ -21,7 +21,7 @@ GROUP = COLS // DOUT
 OPERANDS = 1 + BATCH // GROUP
 LAST_PIECES = 2
 WARM_COLS = 512
-LOAD_BOUNDS = (0, 4, 8, 16, 24, 32)
+LOAD_BOUNDS = (0, 4, 8, 12, 20, 32)
 SPREAD = P // BATCH
 DMA_ALIGN = 4096
 
@@ -50,29 +50,35 @@ def tile_agcrnlayer_pb_t_kernel(tc, adj, cheb2, x, state, r_logit, out):
                     out=unused[:], lhsT=zeros[:, 0:P], rhs=zeros[:], start=True, stop=True
                 )
 
-        keep_warm(5)
+        keep_warm(3)
 
         mat_rows = resident.tile([P, MATS, PACK, NODES], BF16, align_bytes=DMA_ALIGN)
-        for a, matrix in enumerate((adj, cheb2)):
+
+        def load_matrix(a, matrix):
             rows_of = matrix.rearrange("(p r) n -> p r n", r=PACK)
             for half in range(2):
                 pair = slice(2 * half, 2 * half + 2)
                 nc.sync.dma_start(out=mat_rows[:, a, pair], in_=rows_of[:, pair])
         x_flat = resident.tile([P, NODES * DIN], BF16, align_bytes=DMA_ALIGN)
         nc.vector.memset(x_flat[:].bitcast(I32), 0)
-        nc.sync.dma_start(out=x_flat[0:P:SPREAD, :], in_=x.rearrange("b n c -> b (n c)"))
         logit_rows = resident.tile([P, BATCH, PACK, DOUT], BF16, align_bytes=DMA_ALIGN)
         state_rows = resident.tile([P, BATCH, PACK, DOUT], BF16, align_bytes=DMA_ALIGN)
-        for first, behind in zip(LOAD_BOUNDS[:-1], LOAD_BOUNDS[1:]):
-            loaded = slice(first, behind)
+
+        def load_nodes(rows, tensor, loaded):
             nc.sync.dma_start(
-                out=logit_rows[:, loaded],
-                in_=r_logit[loaded].rearrange("b (p t) c -> p b t c", t=PACK),
+                out=rows[:, loaded],
+                in_=tensor[loaded].rearrange("b (p t) c -> p b t c", t=PACK),
             )
-            nc.sync.dma_start(
-                out=state_rows[:, loaded],
-                in_=state[loaded].rearrange("b (p t) c -> p b t c", t=PACK),
-            )
+
+        batches = [slice(first, behind) for first, behind in zip(LOAD_BOUNDS[:-1], LOAD_BOUNDS[1:])]
+        load_matrix(0, adj)
+        load_matrix(1, cheb2)
+        load_nodes(logit_rows, r_logit, batches[0])
+        nc.sync.dma_start(out=x_flat[0:P:SPREAD, :], in_=x.rearrange("b n c -> b (n c)"))
+        load_nodes(state_rows, state, batches[0])
+        for loaded in batches[1:]:
+            load_nodes(logit_rows, r_logit, loaded)
+            load_nodes(state_rows, state, loaded)
 
         ident = resident.tile([P, P], F32)
         masks.make_identity(nc, ident[:])
@@ -212,7 +218,7 @@ def tile_agcrnlayer_pb_t_kernel(tc, adj, cheb2, x, state, r_logit, out):
             else:
                 dst = out_rows[:, stored_batches(i, piece), planes, DIN:FEAT]
                 src = bank[:].rearrange("p q (b c) -> p b q c", c=DOUT)
-            if k % 2 == 0 or (k == 3 and i in (2, 4, 6)):
+            if k % 2 == 0 or (k == 3 and i in (0, 3, 6)):
                 nc.scalar.copy(out=dst, in_=src)
             else:
                 nc.vector.tensor_copy(out=dst, in_=src)
@@ -234,6 +240,7 @@ def tile_agcrnlayer_pb_t_kernel(tc, adj, cheb2, x, state, r_logit, out):
         multiply(1)
         group_x(3, nc.vector.tensor_copy)
         prepare(2)
+        prepare(3)
         quantise(0)
         multiply(0)
         group(2)
@@ -241,7 +248,6 @@ def tile_agcrnlayer_pb_t_kernel(tc, adj, cheb2, x, state, r_logit, out):
             for k in range(BANKS):
                 empty(i, k)
         store(1, 0)
-        prepare(3)
         quantise(2)
         multiply(2)
 

@@ -50,7 +50,7 @@ def tile_agcrnlayer_pb_t_kernel(tc, adj, cheb2, x, state, r_logit, out):
                     out=unused[:], lhsT=zeros[:, 0:P], rhs=zeros[:], start=True, stop=True
                 )
 
-        keep_warm(3)
+        keep_warm(5)
 
         mat_rows = resident.tile([P, MATS, PACK, NODES], BF16, align_bytes=DMA_ALIGN)
 

@@ -21,7 +21,7 @@ GROUP = COLS // DOUT
 OPERANDS = 1 + BATCH // GROUP
 LAST_PIECES = 2
 WARM_COLS = 512
-LOAD_BOUNDS = (0, 4, 8, 12, 20, 32)
+LOAD_BOUNDS = (0, 4, 8, 12, 16, 20, 24, 28, 32)
 SPREAD = P // BATCH
 DMA_ALIGN = 4096
 

import concourse.masks as masks
import concourse.mybir as mybir

F32 = mybir.dt.float32
BF16 = mybir.dt.bfloat16
U32 = mybir.dt.uint32
U8 = mybir.dt.uint8
I32 = mybir.dt.int32
FP8X4 = mybir.dt.float8_e4m3fn_x4

P = 128
PACK = 4
NODES = P * PACK
BATCH = 32
DIN = 8
DOUT = 64
FEAT = DIN + DOUT
MATS = 2
COLS = 256
GROUP = COLS // DOUT
OPERANDS = 1 + BATCH // GROUP
LAST_PIECES = 2
WARM_COLS = 512
LOAD_BOUNDS = (0, 4, 8, 12, 16, 20, 24, 28, 32)
SPREAD = P // BATCH
DMA_ALIGN = 4096

FLOPS = 2 * BATCH * NODES * NODES * MATS * FEAT


def tile_agcrnlayer_pb_t_kernel(tc, adj, cheb2, x, state, r_logit, out):
    nc = tc.nc
    with tc.tile_pool(name="resident", bufs=1) as resident, tc.tile_pool(
        name="rotating", bufs=3
    ) as rotating, tc.psum_pool(name="banks", bufs=8) as banks, tc.manual_schedule():
        warm = resident.tile([P, 1], F32)
        warmed = resident.tile([P, 1], F32)
        nc.gpsimd.memset(warm[:], 0.0)
        nc.scalar.activation(
            out=warmed[:], in_=warm[:], func=mybir.ActivationFunctionType.Sigmoid
        )

        zeros = resident.tile([P, WARM_COLS], BF16)
        nc.vector.memset(zeros[:], 0.0)

        def keep_warm(count):
            unused = banks.tile([P, WARM_COLS], F32, tag="bank")
            for repeat in range(count):
                nc.tensor.matmul(
                    out=unused[:], lhsT=zeros[:, 0:P], rhs=zeros[:], start=True, stop=True
                )

        keep_warm(5)

        mat_rows = resident.tile([P, MATS, PACK, NODES], BF16, align_bytes=DMA_ALIGN)

        def load_matrix(a, matrix):
            rows_of = matrix.rearrange("(p r) n -> p r n", r=PACK)
            for half in range(2):
                pair = slice(2 * half, 2 * half + 2)
                nc.sync.dma_start(out=mat_rows[:, a, pair], in_=rows_of[:, pair])
        x_flat = resident.tile([P, NODES * DIN], BF16, align_bytes=DMA_ALIGN)
        nc.vector.memset(x_flat[:].bitcast(I32), 0)
        logit_rows = resident.tile([P, BATCH, PACK, DOUT], BF16, align_bytes=DMA_ALIGN)
        state_rows = resident.tile([P, BATCH, PACK, DOUT], BF16, align_bytes=DMA_ALIGN)

        def load_nodes(rows, tensor, loaded):
            nc.sync.dma_start(
                out=rows[:, loaded],
                in_=tensor[loaded].rearrange("b (p t) c -> p b t c", t=PACK),
            )

        batches = [slice(first, behind) for first, behind in zip(LOAD_BOUNDS[:-1], LOAD_BOUNDS[1:])]
        load_matrix(0, adj)
        load_matrix(1, cheb2)
        load_nodes(logit_rows, r_logit, batches[0])
        nc.sync.dma_start(out=x_flat[0:P:SPREAD, :], in_=x.rearrange("b n c -> b (n c)"))
        load_nodes(state_rows, state, batches[0])
        for loaded in batches[1:]:
            load_nodes(logit_rows, r_logit, loaded)
            load_nodes(state_rows, state, loaded)

        ident = resident.tile([P, P], F32)
        masks.make_identity(nc, ident[:])
        mat_grouped = resident.tile([P, MATS, NODES, PACK], BF16, align_bytes=64)
        mat_codes = resident.tile([P, MATS, NODES], U32, align_bytes=64)
        mat_scales = resident.tile([P, MATS, NODES], U8, align_bytes=64)
        for a in range(MATS):
            for half in range(2):
                flipped = banks.tile([P, 2, 2 * P], F32, tag="bank")
                for r in (2 * half, 2 * half + 1):
                    words = mat_rows[:, a, r, :].bitcast(F32).rearrange("p (w u) -> p u w", u=2)
                    cols = slice((r % 2) * P, (r % 2 + 1) * P)
                    for u in range(2):
                        nc.tensor.transpose(flipped[:, u, cols], words[:, u, :], ident[:])
                grouped_words = (
                    mat_grouped[:, a, half * 2 * P : (half + 1) * 2 * P, :]
                    .rearrange("p m t -> p (m t)")
                    .bitcast(F32)
                    .rearrange("p (m u) -> p m u", u=2)
                )
                if half == 0:
                    nc.scalar.copy(out=grouped_words, in_=flipped[:].rearrange("p u m -> p m u"))
                else:
                    nc.vector.tensor_copy(
                        out=grouped_words, in_=flipped[:].rearrange("p u m -> p m u")
                    )
            keep_warm(2)
            nc.vector.quantize_mx(
                out=mat_codes[:, a, :].bitcast(FP8X4),
                scales=mat_scales[:, a, :],
                in_=mat_grouped[:, a].rearrange("p m t -> p (m t)"),
            )

        cand_codes = resident.tile([P, OPERANDS, COLS], U32, align_bytes=64)
        cand_scales = resident.tile([P, OPERANDS, COLS], U8, align_bytes=64)
        out_rows = resident.tile(
            [P, BATCH, PACK * MATS, FEAT], F32, align_bytes=DMA_ALIGN
        )
        x_banks = []
        gates = {}
        grouped = {}

        def batches_of(i):
            return slice((i - 1) * GROUP, i * GROUP)

        def prepare(i):
            if i == 0:
                x_words = x_flat[:].bitcast(F32).rearrange(
                    "q (p t w) -> q t w p", t=PACK, w=DIN // 2
                )
                for w in range(DIN // 2):
                    flipped = banks.tile([P, PACK, P], F32, tag="bank")
                    for t in range(PACK):
                        nc.tensor.transpose(flipped[:, t, :], x_words[:, t, w, :], ident[:])
                    x_banks.append(flipped)
                    if w == 1:
                        keep_warm(2)
            else:
                gate = rotating.tile([P, GROUP, DOUT, PACK], F32)
                nc.scalar.activation(
                    out=gate[:],
                    in_=logit_rows[:, batches_of(i)].rearrange("p b t c -> p b c t"),
                    func=mybir.ActivationFunctionType.Sigmoid,
                )
                gates[i] = gate

        x_grouped = resident.tile([P, BATCH, DIN, PACK], BF16, align_bytes=64)
        grouped[0] = x_grouped

        def group_x(w, copy):
            halves = (
                x_banks[w][:]
                .rearrange("p t q -> p (t q)")
                .bitcast(BF16)
                .rearrange("p (t b s e) -> p s b e t", b=BATCH, s=SPREAD, e=2)
            )
            copy(out=x_grouped[:, :, 2 * w : 2 * w + 2, :], in_=halves[:, 0])

        def group(i):
            product = rotating.tile([P, GROUP, DOUT, PACK], BF16, align_bytes=64)
            nc.vector.tensor_tensor(
                out=product[:],
                in0=gates[i][:],
                in1=state_rows[:, batches_of(i)].rearrange("p b t c -> p b c t"),
                op=mybir.AluOpType.mult,
            )
            grouped[i] = product

        def quantise(i):
            nc.vector.quantize_mx(
                out=cand_codes[:, i, :].bitcast(FP8X4),
                scales=cand_scales[:, i, :],
                in_=grouped[i][:].rearrange("p b c t -> p (b c t)"),
            )

        products = {}
        BANKS = PACK

        def pieces_of(i):
            return LAST_PIECES if i == OPERANDS - 1 else 1

        def multiply(i):
            pieces = pieces_of(i)
            width = COLS // pieces
            products[i] = []
            for k in range(BANKS):
                piece, r0 = divmod(k * pieces, PACK)
                cols = slice(piece * width, (piece + 1) * width)
                bank = banks.tile([P, pieces * MATS, width], F32, tag="bank")
                for j in range(pieces):
                    rows = slice((r0 + j) * P, (r0 + j + 1) * P)
                    for a in range(MATS):
                        nc.tensor.matmul_mx(
                            out=bank[:, j * MATS + a, :],
                            lhsT=mat_codes[:, a, rows].bitcast(FP8X4),
                            lhsT_scale=mat_scales[:, a, rows],
                            rhs=cand_codes[:, i, cols].bitcast(FP8X4),
                            rhs_scale=cand_scales[:, i, cols],
                            start=True,
                            stop=True,
                        )
                products[i].append(bank)

        def stored_batches(i, piece):
            count = GROUP // pieces_of(i)
            first = (i - 1) * GROUP + piece * count
            return slice(first, first + count)

        def empty(i, k):
            pieces = pieces_of(i)
            piece, r0 = divmod(k * pieces, PACK)
            bank = products[i][k]
            planes = slice(r0 * MATS, (r0 + pieces) * MATS)
            if i == 0:
                dst = out_rows[:, :, planes, 0:DIN]
                src = bank[:].rearrange("p q (b c) -> p b q c", c=DIN)
            else:
                dst = out_rows[:, stored_batches(i, piece), planes, DIN:FEAT]
                src = bank[:].rearrange("p q (b c) -> p b q c", c=DOUT)
            if k % 2 == 0 or (k == 3 and i in (0, 3, 6)):
                nc.scalar.copy(out=dst, in_=src)
            else:
                nc.vector.tensor_copy(out=dst, in_=src)

        def store(i, piece):
            stored = stored_batches(i, piece)
            nc.sync.dma_start(
                out=out[stored].rearrange("b (p r) a c -> p b (r a c)", r=PACK),
                in_=out_rows[:, stored].rearrange("p b q c -> p b (q c)"),
            )

        prepare(0)
        prepare(1)
        group(1)
        group_x(0, nc.scalar.copy)
        group_x(1, nc.scalar.copy)
        group_x(2, nc.vector.tensor_copy)
        quantise(1)
        multiply(1)
        group_x(3, nc.vector.tensor_copy)
        prepare(2)
        prepare(3)
        quantise(0)
        multiply(0)
        group(2)
        for i in (1, 0):
            for k in range(BANKS):
                empty(i, k)
        store(1, 0)
        quantise(2)
        multiply(2)

        for step in range(3, OPERANDS + 1):
            if step < OPERANDS:
                group(step)
            if step + 1 < OPERANDS:
                prepare(step + 1)
            empty(step - 1, 0)
            empty(step - 1, 1)
            if pieces_of(step - 1) == 2:
                store(step - 1, 0)
            if step < OPERANDS:
                quantise(step)
                multiply(step)
            empty(step - 1, 2)
            empty(step - 1, 3)
            store(step - 1, pieces_of(step - 1) - 1)
